import numpy as np
import ml_dtypes


def mxq(x, axis, fmt="e4m3"):
    dtype, down = {"e4m3": (ml_dtypes.float8_e4m3fn, 7), "e5m2": (ml_dtypes.float8_e5m2, 14)}[fmt]
    v = np.moveaxis(np.asarray(x, np.float32).astype(ml_dtypes.bfloat16).astype(np.float64), axis, -1)
    blocks = v.reshape(v.shape[:-1] + (-1, 32))
    amax = np.abs(blocks).max(-1, keepdims=True)
    byte = np.maximum(np.where(amax > 0, np.frexp(amax)[1] - 1 + 127, 0) - down, 1)
    scale = np.exp2(byte - 127.0)
    codes = (blocks / scale).astype(np.float32).astype(dtype).astype(np.float64)
    return np.moveaxis((codes * scale).reshape(v.shape), -1, axis)


WIDE = False


def mx_kscale(k):
    if not WIDE:
        return np.ones(k)
    levels = np.array([10, -10, 5, -5, 0])
    if k % 512:
        return np.exp2(np.random.permutation(np.resize(levels, k // 32))).repeat(32)
    a = np.empty((k // 512, 16))
    for p in range(k // 512):
        a[p, :8] = np.random.permutation(np.resize(levels, 8))
        for g in range(8):
            far = levels[np.abs(levels - a[p, g]) >= 10]
            a[p, g + 8] = far[np.random.randint(len(far))]
    return np.exp2(a.ravel()).repeat(32)


BF16 = ml_dtypes.bfloat16


def bf(x):
    return np.asarray(x, np.float32).astype(BF16)


def f64(x):
    return np.asarray(x).astype(np.float64)


B, T, D, DI = 4, 256, 1024, 1024
ROPE_BASE = 10000.0


def rotate_half(v):
    h = v.shape[-1] // 2
    return np.concatenate([-v[..., h:], v[..., :h]], axis=-1)


def justnorm(v):
    return v / np.sqrt((v * v).sum(-1, keepdims=True))


def draw0():
    s = mx_kscale(D)
    x = np.random.standard_normal((B, T, D)) * np.exp(0.5 * np.random.standard_normal((B, T, 1)))
    w = justnorm(np.random.uniform(-1.0, 1.0, (2 * DI, D)))
    inv_freq = 1.0 / ROPE_BASE ** (np.arange(0, DI, 2) / DI)
    pos = np.random.randint(0, T) + np.arange(T)
    freqs = pos[:, None] * inv_freq[None, :]
    emb = np.concatenate([freqs, freqs], axis=-1)
    return {"input_vecs": bf(x * s), "qk_w": bf(w / s),
            "sqk": bf(3.0 * (1.0 + 0.2 * np.random.standard_normal(DI)) / np.sqrt(D)),
            "cos": bf(np.cos(emb)), "sin": bf(np.sin(emb))}


def core(input_vecs, qk_w, sqk, cos, sin):
    qk = mxq(f64(input_vecs), 2, "e4m3") @ mxq(f64(qk_w), 1, "e4m3").T
    q, k = np.split(qk, 2, axis=-1)
    c, sn = f64(cos), f64(sin)
    q = q * c + rotate_half(q) * sn
    k = k * c + rotate_half(k) * sn
    sqk_eff = f64(sqk) * np.sqrt(D)
    return justnorm(q) * sqk_eff, justnorm(k) * sqk_eff


def e4m3fn_bytes(y):
    return np.clip(np.asarray(y, np.float64), -448.0, 448.0).astype(np.float32).astype(ml_dtypes.float8_e4m3fn).view(np.uint8)


def e4m3fn_values(b):
    return np.asarray(b, np.uint8).view(ml_dtypes.float8_e4m3fn).astype(np.float64)


def setup_inputs():
    d = draw0()
    x0 = np.asarray(d['qk_w']).astype(np.float64)
    s = (np.max(np.abs(x0), axis=(0,), keepdims=True) / 448.0).astype(np.float32)
    out = {}
    for k, v in d.items():
        if k == 'qk_w':
            out['qk_w_bytes'] = e4m3fn_bytes(x0 / s.astype(np.float64))
            out['qk_w_scale'] = s
        else:
            out[k] = v
    return out


def reference(input_vecs, qk_w_bytes, qk_w_scale, sqk, cos, sin):
    return core(input_vecs, e4m3fn_values(qk_w_bytes) * qk_w_scale.astype(np.float64), sqk, cos, sin)

@@ -1,0 +1,343 @@
+from contextlib import ExitStack
+
+import concourse.mybir as mybir
+from concourse.masks import make_identity
+
+F32 = mybir.dt.float32
+BF16 = mybir.dt.bfloat16
+U32 = mybir.dt.uint32
+U8 = mybir.dt.uint8
+FP8 = mybir.dt.float8_e4m3fn
+FP8X4 = mybir.dt.float8_e4m3fn_x4
+ALU = mybir.AluOpType
+ACT = mybir.ActivationFunctionType
+
+P = 128
+TOK = 1024
+K = 1024
+DI = 1024
+HALF = 512
+FLOPS = 2 * TOK * K * 2 * DI
+
+GM = (2, 0, 1, 2, 2, 0, 0, 1, 0, 1, 0, 0, 0, 1, 0, 0)
+ADD_ON_VECTOR = (15,)
+CAST_ON_VECTOR = (0, 1)
+FIN_LAG = 2
+MANUAL = True
+G_SPLIT = 1
+
+
+def tile_attentionhead_pa_kernel(tc, input_vecs, qk_w_bytes, qk_w_scale, sqk, cos, sin, out_0, out_1):
+    nc = tc.nc
+    x_flat = input_vecs.flatten_outer_dims()
+    outs = (out_0.flatten_outer_dims(), out_1.flatten_outer_dims())
+    w_pairs = qk_w_bytes.rearrange("(c j p) k -> c p j k", j=2, p=P)
+
+    with ExitStack() as ctx:
+        keep = ctx.enter_context(tc.tile_pool(name="keep", bufs=1))
+        cast_pool = ctx.enter_context(tc.tile_pool(name="cast", bufs=3))
+        grp_pool = ctx.enter_context(tc.tile_pool(name="grp", bufs=2))
+        ep_pool = ctx.enter_context(tc.tile_pool(name="ep", bufs=4))
+        st_pool = ctx.enter_context(tc.tile_pool(name="st", bufs=6))
+        tp_pool = ctx.enter_context(tc.psum_pool(name="tp", bufs=2))
+        u_pool = ctx.enter_context(tc.psum_pool(name="up", bufs=2))
+        g_pool = ctx.enter_context(tc.psum_pool(name="gp", bufs=1))
+        if MANUAL:
+            ctx.enter_context(tc.manual_schedule())
+
+        s8 = keep.tile([P, 8], F32, name="s8")
+        wbytes = []
+        x_sb = []
+        for c in range(8):
+            wbytes.append(keep.tile([P, 2, K], U8, name="wbytes%d" % c))
+            x_sb.append(keep.tile([P, K], BF16, name="x_sb%d" % c))
+        cos_t = []
+        sin_t = []
+        for pt in range(2):
+            cos_t.append(keep.tile([P, DI], BF16, name="cos_t%d" % pt))
+            sin_t.append(keep.tile([P, DI], BF16, name="sin_t%d" % pt))
+        gain_row = keep.tile([P, DI], BF16, name="gain_row")
+        gain_sb = keep.tile([P, DI], BF16, name="gain_sb")
+        ones_bf = keep.tile([P, P], BF16, name="ones_bf")
+        ident = keep.tile([P, P], F32, name="ident")
+        warm = keep.tile([P, 1], F32, name="warm")
+        gain_ps = (g_pool.tile([P, HALF], F32, name="gain_ps0"), g_pool.tile([P, HALF], F32, name="gain_ps1"))
+        x_codes = []
+        x_scales = []
+        w_codes = []
+        w_scales = []
+        for c in range(4):
+            x_codes.append(keep.tile([P, 512], U32, name="x_codes%d" % c, align_bytes=64))
+            x_scales.append(keep.tile([P, 512], U8, name="x_scales%d" % c, align_bytes=64))
+            w_codes.append(keep.tile([P, 1024], U32, name="w_codes%d" % c, align_bytes=64))
+            w_scales.append(keep.tile([P, 1024], U8, name="w_scales%d" % c, align_bytes=64))
+
+        nc.vector.memset(warm[:], 1.0)
+        nc.vector.memset(gain_row[:], 0.0)
+        nc.vector.memset(ones_bf[:], 1.0)
+        make_identity(nc, ident[:])
+        nc.scalar.dma_start(
+            out=s8[:].rearrange("p (g t) -> p g t", t=4), in_=qk_w_scale.rearrange("o (g p t) -> p (o g) t", p=P, t=4)
+        )
+        nc.scalar.dma_start(out=gain_row[0:1, :], in_=sqk.rearrange("(o n) -> o n", o=1))
+        nc.scalar.activation(out=warm[:], in_=warm[:], func=ACT.Abs_reciprocal_sqrt)
+
+        def load_w(c):
+            nc.sync.dma_start(out=wbytes[c][:], in_=w_pairs[c])
+
+        def load_x(i):
+            nc.sync.dma_start(out=x_sb[i][:], in_=x_flat[P * i : P * (i + 1), :])
+
+        load_w(0)
+        load_x(0)
+        load_w(1)
+        load_x(1)
+        load_w(2)
+        load_x(2)
+        load_w(3)
+        load_x(3)
+        for i in range(4, 8):
+            load_x(i)
+        for pt in range(2):
+            nc.sync.dma_start(out=cos_t[pt][:], in_=cos[P * pt : P * (pt + 1), :])
+            nc.sync.dma_start(out=sin_t[pt][:], in_=sin[P * pt : P * (pt + 1), :])
+        for c in range(4):
+            load_w(4 + c)
+
+        xg_tiles = {}
+        x_banks = {}
+
+        def turn_x(i):
+            words = x_sb[i][:].bitcast(F32)
+            bank = u_pool.tile([P, 2, 2, P], F32, tag=("u_lo", "u_hi")[i % 2])
+            for g in range(2):
+                for u in range(2):
+                    nc.tensor.transpose(bank[:, g, u, :], words[:, 256 * g + u : 256 * (g + 1) : 2], ident[:])
+            x_banks[i] = bank
+
+        def evac_x(i):
+            if i % 2 == 0:
+                xg = grp_pool.tile([P, 2048], BF16, tag="xg", align_bytes=64, bufs=2)
+                xg_tiles[i // 2] = xg
+            nc.scalar.copy(
+                out=xg_tiles[i // 2][:, 1024 * (i % 2) : 1024 * (i % 2 + 1)]
+                .bitcast(F32)
+                .rearrange("p (g r u) -> p g r u", g=2, u=2),
+                in_=x_banks[i][:].rearrange("p g u r -> p g r u"),
+            )
+
+        def quant_x(pair):
+            nc.vector.quantize_mx(out=x_codes[pair][:].bitcast(FP8X4), scales=x_scales[pair][:], in_=xg_tiles[pair][:])
+
+        wbf_tiles = {}
+        w_banks = {}
+        wg_tiles = {}
+
+        def cast_w(c):
+            wbf = cast_pool.tile([P, 2, K], BF16, tag="wbf")
+            if c in CAST_ON_VECTOR:
+                nc.vector.tensor_copy(out=wbf[:], in_=wbytes[c][:].bitcast(FP8))
+            else:
+                nc.scalar.copy(out=wbf[:], in_=wbytes[c][:].bitcast(FP8))
+            wbf_tiles[c] = wbf
+
+        def turn_w(c, g):
+            words = wbf_tiles[c][:].rearrange("p j k -> p (j k)").bitcast(F32).rearrange("p (j w) -> p j w", j=2)
+            bank = tp_pool.tile([P, 2, 2, P], F32, tag="bank")
+            for u in range(2):
+                for jj in range(2):
+                    nc.tensor.transpose(bank[:, u, jj, :], words[:, jj, 256 * g + u : 256 * (g + 1) : 2], ident[:])
+            w_banks[(c, g)] = bank
+
+        def scale_w(c, g):
+            chunk, pos = divmod(c, 2)
+            if pos == 0 and g == 0:
+                wg = grp_pool.tile([P, 4096], BF16, tag="wg", align_bytes=64, bufs=2)
+                wg_tiles[chunk] = wg
+            src = w_banks[(c, g)][:].rearrange("p u j r -> p (u j r)").bitcast(BF16)
+            dst = wg_tiles[chunk][:].rearrange("p (g n t) -> p g n t", g=2, t=4)
+            nc.vector.tensor_tensor(
+                out=dst[:, g, 256 * pos : 256 * (pos + 1), :].rearrange("p n (u e) -> p n u e", u=2),
+                in0=src.rearrange("p (u n e) -> p n u e", u=2, e=2),
+                in1=s8[:, 4 * g : 4 * (g + 1)].rearrange("p (u e) -> p u e", u=2).unsqueeze(1).to_broadcast([P, 256, 2, 2]),
+                op=ALU.mult,
+            )
+
+        def quant_w(chunk):
+            nc.vector.quantize_mx(out=w_codes[chunk][:].bitcast(FP8X4), scales=w_scales[chunk][:], in_=wg_tiles[chunk][:])
+
+        u_tiles = {}
+
+        def mm(n):
+            h, i = divmod(n, 8)
+            u_lo = u_pool.tile([P, HALF], F32, tag="u_lo")
+            u_hi = u_pool.tile([P, HALF], F32, tag="u_hi")
+            u_tiles[n] = (u_lo, u_hi)
+            for half in range(2):
+                for g in range(2):
+                    nc.tensor.matmul_mx(
+                        out=u_tiles[n][half][:],
+                        lhsT=x_codes[i // 2][:, 256 * (i % 2) + P * g : 256 * (i % 2) + P * (g + 1)].bitcast(FP8X4),
+                        lhsT_scale=x_scales[i // 2][:, 256 * (i % 2) + P * g : 256 * (i % 2) + P * (g + 1)],
+                        rhs=w_codes[2 * h + half][:, HALF * g : HALF * (g + 1)].bitcast(FP8X4),
+                        rhs_scale=w_scales[2 * h + half][:, HALF * g : HALF * (g + 1)],
+                        start=(g == 0),
+                        stop=(g == 1),
+                    )
+
+        r_tiles = {}
+        rg_tiles = {}
+        rn_tiles = {}
+        o_tiles = {}
+
+        def rope(n):
+            pt = n % 2
+            u_lo, u_hi = u_tiles[n]
+            a = ep_pool.tile([P, DI], F32, tag="a", bufs=5)
+            b = ep_pool.tile([P, DI], F32, tag="b", bufs=3)
+            nc.vector.tensor_tensor(out=a[:, 0:HALF], in0=u_lo[:], in1=cos_t[pt][:, 0:HALF], op=ALU.mult)
+            nc.vector.tensor_tensor(out=b[:, HALF:DI], in0=u_lo[:], in1=sin_t[pt][:, HALF:DI], op=ALU.mult)
+            nc.vector.tensor_tensor(out=a[:, HALF:DI], in0=u_hi[:], in1=cos_t[pt][:, HALF:DI], op=ALU.mult)
+            nc.vector.scalar_tensor_tensor(
+                out=b[:, 0:HALF], in0=u_hi[:], scalar=-1.0, in1=sin_t[pt][:, 0:HALF], op0=ALU.mult, op1=ALU.mult
+            )
+            if n in ADD_ON_VECTOR:
+                nc.vector.tensor_tensor(out=a[:], in0=a[:], in1=b[:], op=ALU.add)
+            else:
+                for s in range(G_SPLIT):
+                    cols = slice(DI // G_SPLIT * s, DI // G_SPLIT * (s + 1))
+                    nc.gpsimd.tensor_tensor(out=a[:, cols], in0=a[:, cols], in1=b[:, cols], op=ALU.add)
+            r_tiles[n] = a
+            if GM[n] > 0:
+                rg = ep_pool.tile([P, DI], F32, tag="rg", bufs=3)
+                cols = slice(DI - HALF * GM[n], DI)
+                nc.gpsimd.tensor_tensor(out=rg[:, cols], in0=a[:, cols], in1=gain_sb[:, cols], op=ALU.mult)
+                rg_tiles[n] = rg
+
+        def norm(n):
+            junk = ep_pool.tile([P, DI], BF16, tag="junk", bufs=2)
+            ss = st_pool.tile([P, 1], F32, tag="ss")
+            rn = st_pool.tile([P, 1], F32, tag="rn")
+            nc.scalar.activation(out=junk[:], in_=r_tiles[n][:], func=ACT.Square, accum_out=ss[:])
+            nc.scalar.activation(out=rn[:], in_=ss[:], func=ACT.Abs_reciprocal_sqrt, scale=1.0 / 1024.0)
+            rn_tiles[n] = rn
+
+        def finish_scalar(n):
+            o = ep_pool.tile([P, DI], F32, tag="o", bufs=3)
+            o_tiles[n] = o
+            if GM[n] > 0:
+                lo = DI - HALF * GM[n]
+                nc.scalar.activation(
+                    out=o[:, lo:DI], in_=rg_tiles[n][:, lo:DI], func=ACT.Copy, scale=rn_tiles[n][:, 0:1]
+                )
+
+        def finish_vector(n):
+            h, i = divmod(n, 8)
+            rows = slice(P * i, P * (i + 1))
+            o = o_tiles[n]
+            for s in range(2 - GM[n]):
+                cols = slice(HALF * s, HALF * (s + 1))
+                nc.vector.scalar_tensor_tensor(
+                    out=o[:, cols], in0=r_tiles[n][:, cols], scalar=rn_tiles[n][:, 0:1], in1=gain_ps[s][:],
+                    op0=ALU.mult, op1=ALU.mult,
+                )
+            if n >= 14:
+                for s in range(2):
+                    cols = slice(HALF * s, HALF * (s + 1))
+                    nc.sync.dma_start(out=outs[h][rows, cols], in_=o[:, cols])
+            else:
+                nc.sync.dma_start(out=outs[h][rows, :], in_=o[:])
+
+        jobs = []
+
+        def job_x(i):
+            jobs.append((lambda: turn_x(i), lambda: evac_x(i)))
+
+        def job_w(c, g):
+            jobs.append((lambda: turn_w(c, g), lambda: scale_w(c, g)))
+
+        for c in range(8):
+            job_w(c, 0)
+            job_w(c, 1)
+        state = {"made": 0, "used": 0}
+
+        def make():
+            if state["made"] < len(jobs):
+                jobs[state["made"]][0]()
+                state["made"] = state["made"] + 1
+
+        def advance(count):
+            for q in range(count):
+                jobs[state["used"]][1]()
+                state["used"] = state["used"] + 1
+                make()
+
+        def prep_x(i):
+            turn_x(i)
+            evac_x(i)
+
+        cast_w(0)
+        turn_x(0)
+        make()
+        make()
+        evac_x(0)
+        cast_w(1)
+        prep_x(1)
+        cast_w(2)
+        advance(2)
+        prep_x(2)
+        cast_w(3)
+        advance(1)
+        quant_x(0)
+        prep_x(3)
+        advance(1)
+        prep_x(4)
+        cast_w(4)
+        advance(1)
+        quant_w(0)
+        prep_x(5)
+        advance(1)
+        quant_x(1)
+        prep_x(6)
+        for s in range(2):
+            nc.tensor.matmul(
+                out=gain_ps[s][:], lhsT=ones_bf[:], rhs=gain_row[:, HALF * s : HALF * (s + 1)], start=True, stop=True
+            )
+        advance(1)
+        quant_x(2)
+        prep_x(7)
+        advance(1)
+        cast_w(5)
+        for s in range(2):
+            nc.scalar.copy(out=gain_sb[:, HALF * s : HALF * (s + 1)], in_=gain_ps[s][:])
+        quant_w(1)
+        mm(0)
+        quant_x(3)
+        mm(1)
+
+        post = (2, 1, 1, 1, 1, 2)
+        for n in range(16):
+            f = n - FIN_LAG
+            if f >= 0:
+                finish_scalar(f)
+            if n == 1:
+                cast_w(6)
+            if n == 3:
+                cast_w(7)
+            rope(n)
+            if n == 6:
+                quant_w(3)
+            if n + 2 < 16:
+                mm(n + 2)
+            if f >= 0:
+                finish_vector(f)
+            if n < 6:
+                advance(post[n])
+            if n >= 1:
+                norm(n - 1)
+            if n == 3:
+                quant_w(2)
+        norm(15)
+        for n in range(16 - FIN_LAG, 16):
+            finish_scalar(n)
+            finish_vector(n)

@@ -19,12 +19,14 @@ DI = 1024
 HALF = 512
 FLOPS = 2 * TOK * K * 2 * DI
 
-GM = (2, 0, 1, 2, 2, 0, 0, 1, 0, 1, 0, 0, 0, 1, 0, 0)
+GM = (1, 1, 1, 1, 1, 1, 1, 0, 0, 0, 0, 0, 0, 0, 0, 0)
 ADD_ON_VECTOR = (15,)
 CAST_ON_VECTOR = (0, 1)
 FIN_LAG = 2
 MANUAL = True
 G_SPLIT = 1
+TS = (1, 1, 1, 1, 1, 1, 1, 1, 1, 1, 1, 1, 1, 1, 0, 0)
+LAST_EARLY = 4
 
 
 def tile_attentionhead_pa_kernel(tc, input_vecs, qk_w_bytes, qk_w_scale, sqk, cos, sin, out_0, out_1):
@@ -61,7 +63,17 @@ def tile_attentionhead_pa_kernel(tc, input_vecs, qk_w_bytes, qk_w_scale, sqk, co
         ones_bf = keep.tile([P, P], BF16, name="ones_bf")
         ident = keep.tile([P, P], F32, name="ident")
         warm = keep.tile([P, 1], F32, name="warm")
-        gain_ps = (g_pool.tile([P, HALF], F32, name="gain_ps0"), g_pool.tile([P, HALF], F32, name="gain_ps1"))
+        gain_t = keep.tile([P, 8], F32, name="gain_t")
+        gain_ps = {}
+
+        def spread_gain():
+            for s in range(2):
+                bank = g_pool.tile([P, HALF], F32, tag="g%d" % s)
+                gain_ps[s] = bank
+                nc.tensor.matmul(
+                    out=gain_ps[s][:], lhsT=ones_bf[:], rhs=gain_row[:, HALF * s : HALF * (s + 1)], start=True, stop=True
+                )
+
         x_codes = []
         x_scales = []
         w_codes = []
@@ -223,7 +235,7 @@ def tile_attentionhead_pa_kernel(tc, input_vecs, qk_w_bytes, qk_w_scale, sqk, co
             rn_tiles[n] = rn
 
         def finish_scalar(n):
-            o = ep_pool.tile([P, DI], F32, tag="o", bufs=3)
+            o = ep_pool.tile([P, DI], F32, tag="o", bufs=4)
             o_tiles[n] = o
             if GM[n] > 0:
                 lo = DI - HALF * GM[n]
@@ -231,16 +243,69 @@ def tile_attentionhead_pa_kernel(tc, input_vecs, qk_w_bytes, qk_w_scale, sqk, co
                     out=o[:, lo:DI], in_=rg_tiles[n][:, lo:DI], func=ACT.Copy, scale=rn_tiles[n][:, 0:1]
                 )
 
+        t1_banks = {}
+        t2_banks = {}
+        rgt_tiles = {}
+
+        def build_gain_t():
+            bank = g_pool.tile([P, 8], F32, tag="g0")
+            for c in range(8):
+                nc.tensor.matmul(
+                    out=bank[:, c : c + 1], lhsT=gain_row[:, P * c : P * (c + 1)], rhs=ones_bf[:, 0:1], start=True, stop=True
+                )
+            nc.scalar.copy(out=gain_t[:], in_=bank[:])
+
+        def t1(n):
+            for s in range(TS[n]):
+                if n <= LAST_EARLY:
+                    bank = g_pool.tile([P, 4, P], F32, tag="g0")
+                else:
+                    bank = tp_pool.tile([P, 4, P], F32, tag="bank")
+                for c in range(4):
+                    nc.tensor.transpose(bank[:, c, :], r_tiles[n][:, HALF * s + P * c : HALF * s + P * (c + 1)], ident[:])
+                t1_banks[(n, s)] = bank
+
+        def e1(n):
+            for s in range(TS[n]):
+                rgt = ep_pool.tile([P, 4, P], F32, tag="rgt", bufs=2)
+                for c in range(4):
+                    nc.scalar.activation(
+                        out=rgt[:, c, :], in_=t1_banks[(n, s)][:, c, :], func=ACT.Copy, scale=gain_t[:, 4 * s + c : 4 * s + c + 1]
+                    )
+                rgt_tiles[(n, s)] = rgt
+
+        def t2(n):
+            for s in range(TS[n]):
+                if n <= LAST_EARLY:
+                    bank = g_pool.tile([P, 4, P], F32, tag="g1")
+                else:
+                    bank = tp_pool.tile([P, 4, P], F32, tag="bank")
+                for c in range(4):
+                    nc.tensor.transpose(bank[:, c, :], rgt_tiles[(n, s)][:, c, :], ident[:])
+                t2_banks[(n, s)] = bank
+
+        def e2(n):
+            for s in range(TS[n]):
+                nc.scalar.activation(
+                    out=o_tiles[n][:, HALF * s : HALF * (s + 1)],
+                    in_=t2_banks[(n, s)][:].rearrange("p c r -> p (c r)"),
+                    func=ACT.Copy,
+                    scale=rn_tiles[n][:, 0:1],
+                )
+
         def finish_vector(n):
-            h, i = divmod(n, 8)
-            rows = slice(P * i, P * (i + 1))
             o = o_tiles[n]
-            for s in range(2 - GM[n]):
+            for s in range(TS[n], 2 - GM[n]):
                 cols = slice(HALF * s, HALF * (s + 1))
                 nc.vector.scalar_tensor_tensor(
                     out=o[:, cols], in0=r_tiles[n][:, cols], scalar=rn_tiles[n][:, 0:1], in1=gain_ps[s][:],
                     op0=ALU.mult, op1=ALU.mult,
                 )
+
+        def store(n):
+            h, i = divmod(n, 8)
+            rows = slice(P * i, P * (i + 1))
+            o = o_tiles[n]
             if n >= 14:
                 for s in range(2):
                     cols = slice(HALF * s, HALF * (s + 1))
@@ -299,10 +364,7 @@ def tile_attentionhead_pa_kernel(tc, input_vecs, qk_w_bytes, qk_w_scale, sqk, co
         advance(1)
         quant_x(1)
         prep_x(6)
-        for s in range(2):
-            nc.tensor.matmul(
-                out=gain_ps[s][:], lhsT=ones_bf[:], rhs=gain_row[:, HALF * s : HALF * (s + 1)], start=True, stop=True
-            )
+        spread_gain()
         advance(1)
         quant_x(2)
         prep_x(7)
@@ -314,6 +376,7 @@ def tile_attentionhead_pa_kernel(tc, input_vecs, qk_w_bytes, qk_w_scale, sqk, co
         mm(0)
         quant_x(3)
         mm(1)
+        build_gain_t()
 
         post = (2, 1, 1, 1, 1, 2)
         for n in range(16):
@@ -327,6 +390,8 @@ def tile_attentionhead_pa_kernel(tc, input_vecs, qk_w_bytes, qk_w_scale, sqk, co
             rope(n)
             if n == 6:
                 quant_w(3)
+            if n >= 1:
+                t1(n - 1)
             if n + 2 < 16:
                 mm(n + 2)
             if f >= 0:
@@ -335,9 +400,18 @@ def tile_attentionhead_pa_kernel(tc, input_vecs, qk_w_bytes, qk_w_scale, sqk, co
                 advance(post[n])
             if n >= 1:
                 norm(n - 1)
+            if f >= 0:
+                e2(f)
+                store(f)
+            if n >= 1:
+                e1(n - 1)
+                t2(n - 1)
+            if f == LAST_EARLY:
+                spread_gain()
             if n == 3:
                 quant_w(2)
         norm(15)
         for n in range(16 - FIN_LAG, 16):
             finish_scalar(n)
             finish_vector(n)
+            store(n)

@@ -26,7 +26,7 @@ FIN_LAG = 2
 MANUAL = True
 G_SPLIT = 1
 TS = (1, 1, 1, 1, 1, 1, 1, 1, 1, 1, 1, 1, 1, 1, 0, 0)
-LAST_EARLY = 4
+LAST_EARLY = 5
 
 
 def tile_attentionhead_pa_kernel(tc, input_vecs, qk_w_bytes, qk_w_scale, sqk, cos, sin, out_0, out_1):
@@ -74,6 +74,16 @@ def tile_attentionhead_pa_kernel(tc, input_vecs, qk_w_bytes, qk_w_scale, sqk, co
                     out=gain_ps[s][:], lhsT=ones_bf[:], rhs=gain_row[:, HALF * s : HALF * (s + 1)], start=True, stop=True
                 )
 
+        idle_rhs = keep.tile([P, HALF], BF16, name="idle_rhs")
+        idle_ps = {}
+
+        def keep_clock(count):
+            for j in range(count):
+                if j not in idle_ps:
+                    bank = g_pool.tile([P, HALF], F32, tag="g%d" % j)
+                    idle_ps[j] = bank
+                nc.tensor.matmul(out=idle_ps[j][:], lhsT=ones_bf[:], rhs=idle_rhs[:], start=True, stop=True)
+
         x_codes = []
         x_scales = []
         w_codes = []
@@ -87,6 +97,7 @@ def tile_attentionhead_pa_kernel(tc, input_vecs, qk_w_bytes, qk_w_scale, sqk, co
         nc.vector.memset(warm[:], 1.0)
         nc.vector.memset(gain_row[:], 0.0)
         nc.vector.memset(ones_bf[:], 1.0)
+        nc.vector.memset(idle_rhs[:], 0.0)
         make_identity(nc, ident[:])
         nc.scalar.dma_start(
             out=s8[:].rearrange("p (g t) -> p g t", t=4), in_=qk_w_scale.rearrange("o (g p t) -> p (o g) t", p=P, t=4)
@@ -255,43 +266,56 @@ def tile_attentionhead_pa_kernel(tc, input_vecs, qk_w_bytes, qk_w_scale, sqk, co
                 )
             nc.scalar.copy(out=gain_t[:], in_=bank[:])
 
-        def t1(n):
-            for s in range(TS[n]):
-                if n <= LAST_EARLY:
-                    bank = g_pool.tile([P, 4, P], F32, tag="g0")
-                else:
-                    bank = tp_pool.tile([P, 4, P], F32, tag="bank")
-                for c in range(4):
-                    nc.tensor.transpose(bank[:, c, :], r_tiles[n][:, HALF * s + P * c : HALF * s + P * (c + 1)], ident[:])
-                t1_banks[(n, s)] = bank
+        ts_state = {"count": 1}
 
-        def e1(n):
-            for s in range(TS[n]):
-                rgt = ep_pool.tile([P, 4, P], F32, tag="rgt", bufs=2)
-                for c in range(4):
-                    nc.scalar.activation(
-                        out=rgt[:, c, :], in_=t1_banks[(n, s)][:, c, :], func=ACT.Copy, scale=gain_t[:, 4 * s + c : 4 * s + c + 1]
-                    )
-                rgt_tiles[(n, s)] = rgt
+        def ts_bank(early):
+            if early:
+                k = ts_state["count"] % 2
+                ts_state["count"] = ts_state["count"] + 1
+                bank = g_pool.tile([P, 4, P], F32, tag="g%d" % k)
+            else:
+                bank = tp_pool.tile([P, 4, P], F32, tag="bank")
+            return bank
 
-        def t2(n):
-            for s in range(TS[n]):
-                if n <= LAST_EARLY:
-                    bank = g_pool.tile([P, 4, P], F32, tag="g1")
-                else:
-                    bank = tp_pool.tile([P, 4, P], F32, tag="bank")
-                for c in range(4):
-                    nc.tensor.transpose(bank[:, c, :], rgt_tiles[(n, s)][:, c, :], ident[:])
-                t2_banks[(n, s)] = bank
+        def t1(n, s, early):
+            bank = ts_bank(early)
+            for c in range(4):
+                nc.tensor.transpose(bank[:, c, :], r_tiles[n][:, HALF * s + P * c : HALF * s + P * (c + 1)], ident[:])
+            t1_banks[(n, s)] = bank
 
-        def e2(n):
-            for s in range(TS[n]):
+        def e1(n, s):
+            rgt = ep_pool.tile([P, 4, P], F32, tag="rgt", bufs=4)
+            for c in range(4):
                 nc.scalar.activation(
-                    out=o_tiles[n][:, HALF * s : HALF * (s + 1)],
-                    in_=t2_banks[(n, s)][:].rearrange("p c r -> p (c r)"),
-                    func=ACT.Copy,
-                    scale=rn_tiles[n][:, 0:1],
+                    out=rgt[:, c, :], in_=t1_banks[(n, s)][:, c, :], func=ACT.Copy, scale=gain_t[:, 4 * s + c : 4 * s + c + 1]
                 )
+            rgt_tiles[(n, s)] = rgt
+
+        def t2(n, s, early):
+            bank = ts_bank(early)
+            for c in range(4):
+                nc.tensor.transpose(bank[:, c, :], rgt_tiles[(n, s)][:, c, :], ident[:])
+            t2_banks[(n, s)] = bank
+
+        def e2(n, s):
+            nc.scalar.activation(
+                out=o_tiles[n][:, HALF * s : HALF * (s + 1)],
+                in_=t2_banks[(n, s)][:].rearrange("p c r -> p (c r)"),
+                func=ACT.Copy,
+                scale=rn_tiles[n][:, 0:1],
+            )
+
+        def ts_round(m, f, s, early):
+            do1 = m >= 0 and s < TS[m]
+            do2 = f >= 0 and s < TS[f]
+            if do1:
+                t1(m, s, early)
+            if do2:
+                t2(f, s, early)
+            if do1:
+                e1(m, s)
+            if do2:
+                e2(f, s)
 
         def finish_vector(n):
             o = o_tiles[n]
@@ -338,9 +362,12 @@ def tile_attentionhead_pa_kernel(tc, input_vecs, qk_w_bytes, qk_w_scale, sqk, co
                 make()
 
         def prep_x(i):
+            if i <= 6:
+                keep_clock(2)
             turn_x(i)
             evac_x(i)
 
+        keep_clock(2)
         cast_w(0)
         turn_x(0)
         make()
@@ -391,23 +418,19 @@ def tile_attentionhead_pa_kernel(tc, input_vecs, qk_w_bytes, qk_w_scale, sqk, co
             if n == 6:
                 quant_w(3)
             if n >= 1:
-                t1(n - 1)
+                norm(n - 1)
+            ts_round(n - 1, f, 0, n <= LAST_EARLY)
             if n + 2 < 16:
                 mm(n + 2)
+            ts_round(n - 1, f, 1, n <= LAST_EARLY)
+            if n == LAST_EARLY + 1:
+                spread_gain()
             if f >= 0:
                 finish_vector(f)
             if n < 6:
                 advance(post[n])
-            if n >= 1:
-                norm(n - 1)
             if f >= 0:
-                e2(f)
                 store(f)
-            if n >= 1:
-                e1(n - 1)
-                t2(n - 1)
-            if f == LAST_EARLY:
-                spread_gain()
             if n == 3:
                 quant_w(2)
         norm(15)

@@ -19,7 +19,7 @@ DI = 1024
 HALF = 512
 FLOPS = 2 * TOK * K * 2 * DI
 
-GM = (1, 1, 1, 1, 1, 1, 1, 0, 0, 0, 0, 0, 0, 0, 0, 0)
+GM = (1, 1, 1, 1, 1, 0, 0, 0, 0, 0, 0, 0, 0, 0, 0, 0)
 ADD_ON_VECTOR = (15,)
 CAST_ON_VECTOR = (0, 1)
 FIN_LAG = 2
@@ -37,7 +37,7 @@ def tile_attentionhead_pa_kernel(tc, input_vecs, qk_w_bytes, qk_w_scale, sqk, co
 
     with ExitStack() as ctx:
         keep = ctx.enter_context(tc.tile_pool(name="keep", bufs=1))
-        cast_pool = ctx.enter_context(tc.tile_pool(name="cast", bufs=3))
+        cast_pool = ctx.enter_context(tc.tile_pool(name="cast", bufs=4))
         grp_pool = ctx.enter_context(tc.tile_pool(name="grp", bufs=2))
         ep_pool = ctx.enter_context(tc.tile_pool(name="ep", bufs=4))
         st_pool = ctx.enter_context(tc.tile_pool(name="st", bufs=6))
@@ -404,17 +404,18 @@ def tile_attentionhead_pa_kernel(tc, input_vecs, qk_w_bytes, qk_w_scale, sqk, co
         quant_x(3)
         mm(1)
         build_gain_t()
+        cast_w(6)
 
-        post = (2, 1, 1, 1, 1, 2)
+        post = (1, 2, 1, 1, 1, 2)
         for n in range(16):
             f = n - FIN_LAG
             if f >= 0:
                 finish_scalar(f)
             if n == 1:
-                cast_w(6)
-            if n == 3:
                 cast_w(7)
             rope(n)
+            if n == 4:
+                quant_w(2)
             if n == 6:
                 quant_w(3)
             if n >= 1:
@@ -431,8 +432,6 @@ def tile_attentionhead_pa_kernel(tc, input_vecs, qk_w_bytes, qk_w_scale, sqk, co
                 advance(post[n])
             if f >= 0:
                 store(f)
-            if n == 3:
-                quant_w(2)
         norm(15)
         for n in range(16 - FIN_LAG, 16):
             finish_scalar(n)

@@ -19,13 +19,13 @@ DI = 1024
 HALF = 512
 FLOPS = 2 * TOK * K * 2 * DI
 
-GM = (1, 1, 1, 1, 1, 0, 0, 0, 0, 0, 0, 0, 0, 0, 0, 0)
+GM = (1, 1, 1, 1, 0, 0, 0, 0, 0, 0, 0, 0, 0, 0, 0, 0)
 ADD_ON_VECTOR = (15,)
 CAST_ON_VECTOR = (0, 1)
 FIN_LAG = 2
 MANUAL = True
 G_SPLIT = 1
-TS = (1, 1, 1, 1, 1, 1, 1, 1, 1, 1, 1, 1, 1, 1, 0, 0)
+TS = (1, 1, 1, 1, 2, 2, 1, 1, 1, 1, 1, 1, 1, 1, 0, 0)
 LAST_EARLY = 5
 
 
@@ -114,10 +114,10 @@ def tile_attentionhead_pa_kernel(tc, input_vecs, qk_w_bytes, qk_w_scale, sqk, co
         load_w(0)
         load_x(0)
         load_w(1)
-        load_x(1)
         load_w(2)
-        load_x(2)
+        load_x(1)
         load_w(3)
+        load_x(2)
         load_x(3)
         for i in range(4, 8):
             load_x(i)
@@ -374,31 +374,28 @@ def tile_attentionhead_pa_kernel(tc, input_vecs, qk_w_bytes, qk_w_scale, sqk, co
         make()
         evac_x(0)
         cast_w(1)
-        prep_x(1)
         cast_w(2)
+        prep_x(1)
         advance(2)
-        prep_x(2)
         cast_w(3)
+        prep_x(2)
         advance(1)
         quant_x(0)
         prep_x(3)
         advance(1)
-        prep_x(4)
-        cast_w(4)
-        advance(1)
         quant_w(0)
+        cast_w(4)
+        prep_x(4)
         prep_x(5)
-        advance(1)
+        advance(2)
         quant_x(1)
         prep_x(6)
         spread_gain()
-        advance(1)
-        quant_x(2)
         prep_x(7)
-        advance(1)
+        advance(2)
         cast_w(5)
-        for s in range(2):
-            nc.scalar.copy(out=gain_sb[:, HALF * s : HALF * (s + 1)], in_=gain_ps[s][:])
+        nc.scalar.copy(out=gain_sb[:, HALF:DI], in_=gain_ps[1][:])
+        quant_x(2)
         quant_w(1)
         mm(0)
         quant_x(3)

@@ -19,13 +19,13 @@ DI = 1024
 HALF = 512
 FLOPS = 2 * TOK * K * 2 * DI
 
-GM = (1, 1, 1, 1, 0, 0, 0, 0, 0, 0, 0, 0, 0, 0, 0, 0)
+GM = (1, 1, 1, 1, 1, 0, 0, 0, 0, 0, 0, 0, 0, 0, 0, 0)
 ADD_ON_VECTOR = (15,)
 CAST_ON_VECTOR = (0, 1)
 FIN_LAG = 2
 MANUAL = True
 G_SPLIT = 1
-TS = (1, 1, 1, 1, 2, 2, 1, 1, 1, 1, 1, 1, 1, 1, 0, 0)
+TS = (1, 1, 1, 1, 1, 1, 1, 1, 1, 1, 1, 1, 1, 1, 0, 0)
 LAST_EARLY = 5
 
 

@@ -20,12 +20,10 @@ HALF = 512
 FLOPS = 2 * TOK * K * 2 * DI
 
 GM = (1, 1, 1, 1, 1, 0, 0, 0, 0, 0, 0, 0, 0, 0, 0, 0)
-ADD_ON_VECTOR = (15,)
 CAST_ON_VECTOR = (0, 1)
 FIN_LAG = 2
 MANUAL = True
-G_SPLIT = 1
-TS = (1, 1, 1, 1, 1, 1, 1, 1, 1, 1, 1, 1, 1, 1, 0, 0)
+TS = (1, 1, 1, 1, 1, 1, 1, 1, 1, 1, 1, 1, 1, 0, 0, 0)
 LAST_EARLY = 5
 
 
@@ -218,18 +216,23 @@ def tile_attentionhead_pa_kernel(tc, input_vecs, qk_w_bytes, qk_w_scale, sqk, co
             u_lo, u_hi = u_tiles[n]
             a = ep_pool.tile([P, DI], F32, tag="a", bufs=5)
             b = ep_pool.tile([P, DI], F32, tag="b", bufs=3)
-            nc.vector.tensor_tensor(out=a[:, 0:HALF], in0=u_lo[:], in1=cos_t[pt][:, 0:HALF], op=ALU.mult)
-            nc.vector.tensor_tensor(out=b[:, HALF:DI], in0=u_lo[:], in1=sin_t[pt][:, HALF:DI], op=ALU.mult)
-            nc.vector.tensor_tensor(out=a[:, HALF:DI], in0=u_hi[:], in1=cos_t[pt][:, HALF:DI], op=ALU.mult)
-            nc.vector.scalar_tensor_tensor(
-                out=b[:, 0:HALF], in0=u_hi[:], scalar=-1.0, in1=sin_t[pt][:, 0:HALF], op0=ALU.mult, op1=ALU.mult
-            )
-            if n in ADD_ON_VECTOR:
-                nc.vector.tensor_tensor(out=a[:], in0=a[:], in1=b[:], op=ALU.add)
+            lo, hi = slice(0, HALF), slice(HALF, DI)
+            nc.vector.tensor_tensor(out=a[:, lo], in0=u_lo[:], in1=cos_t[pt][:, lo], op=ALU.mult)
+            if n == 15:
+                nc.vector.scalar_tensor_tensor(
+                    out=b[:, lo], in0=u_hi[:], scalar=-1.0, in1=sin_t[pt][:, lo], op0=ALU.mult, op1=ALU.mult
+                )
+                nc.vector.tensor_tensor(out=a[:, hi], in0=u_hi[:], in1=cos_t[pt][:, hi], op=ALU.mult)
+                nc.vector.tensor_tensor(out=b[:, hi], in0=u_lo[:], in1=sin_t[pt][:, hi], op=ALU.mult)
+                for half in (lo, hi):
+                    nc.vector.tensor_tensor(out=a[:, half], in0=a[:, half], in1=b[:, half], op=ALU.add)
             else:
-                for s in range(G_SPLIT):
-                    cols = slice(DI // G_SPLIT * s, DI // G_SPLIT * (s + 1))
-                    nc.gpsimd.tensor_tensor(out=a[:, cols], in0=a[:, cols], in1=b[:, cols], op=ALU.add)
+                nc.vector.tensor_tensor(out=b[:, hi], in0=u_lo[:], in1=sin_t[pt][:, hi], op=ALU.mult)
+                nc.vector.tensor_tensor(out=a[:, hi], in0=u_hi[:], in1=cos_t[pt][:, hi], op=ALU.mult)
+                nc.vector.scalar_tensor_tensor(
+                    out=b[:, lo], in0=u_hi[:], scalar=-1.0, in1=sin_t[pt][:, lo], op0=ALU.mult, op1=ALU.mult
+                )
+                nc.gpsimd.tensor_tensor(out=a[:], in0=a[:], in1=b[:], op=ALU.add)
             r_tiles[n] = a
             if GM[n] > 0:
                 rg = ep_pool.tile([P, DI], F32, tag="rg", bufs=3)
@@ -239,10 +242,21 @@ def tile_attentionhead_pa_kernel(tc, input_vecs, qk_w_bytes, qk_w_scale, sqk, co
 
         def norm(n):
             junk = ep_pool.tile([P, DI], BF16, tag="junk", bufs=2)
-            ss = st_pool.tile([P, 1], F32, tag="ss")
             rn = st_pool.tile([P, 1], F32, tag="rn")
-            nc.scalar.activation(out=junk[:], in_=r_tiles[n][:], func=ACT.Square, accum_out=ss[:])
-            nc.scalar.activation(out=rn[:], in_=ss[:], func=ACT.Abs_reciprocal_sqrt, scale=1.0 / 1024.0)
+            if n == 15:
+                ss = st_pool.tile([P, 2], F32, tag="ss2", bufs=1)
+                for s in range(2):
+                    cols = slice(HALF * s, HALF * (s + 1))
+                    nc.scalar.activation(
+                        out=junk[:, cols], in_=r_tiles[n][:, cols], func=ACT.Square, scale=1.0 / 32.0, accum_out=ss[:, s : s + 1]
+                    )
+                nc.scalar.activation(
+                    out=rn[:], in_=ss[:, 0:1], func=ACT.Abs_reciprocal_sqrt, bias=ss[:, 1:2], scale=1.0
+                )
+            else:
+                ss = st_pool.tile([P, 1], F32, tag="ss")
+                nc.scalar.activation(out=junk[:], in_=r_tiles[n][:], func=ACT.Square, accum_out=ss[:])
+                nc.scalar.activation(out=rn[:], in_=ss[:], func=ACT.Abs_reciprocal_sqrt, scale=1.0 / 1024.0)
             rn_tiles[n] = rn
 
         def finish_scalar(n):

from contextlib import ExitStack

import concourse.mybir as mybir
from concourse.masks import make_identity

F32 = mybir.dt.float32
BF16 = mybir.dt.bfloat16
U32 = mybir.dt.uint32
U8 = mybir.dt.uint8
FP8 = mybir.dt.float8_e4m3fn
FP8X4 = mybir.dt.float8_e4m3fn_x4
ALU = mybir.AluOpType
ACT = mybir.ActivationFunctionType

P = 128
TOK = 1024
K = 1024
DI = 1024
HALF = 512
FLOPS = 2 * TOK * K * 2 * DI

GM = (1, 1, 1, 1, 1, 0, 0, 0, 0, 0, 0, 0, 0, 0, 0, 0)
CAST_ON_VECTOR = (0, 1)
FIN_LAG = 2
MANUAL = True
TS = (1, 1, 1, 1, 1, 1, 1, 1, 1, 1, 1, 1, 1, 0, 0, 0)
LAST_EARLY = 5


def tile_attentionhead_pa_kernel(tc, input_vecs, qk_w_bytes, qk_w_scale, sqk, cos, sin, out_0, out_1):
    nc = tc.nc
    x_flat = input_vecs.flatten_outer_dims()
    outs = (out_0.flatten_outer_dims(), out_1.flatten_outer_dims())
    w_pairs = qk_w_bytes.rearrange("(c j p) k -> c p j k", j=2, p=P)

    with ExitStack() as ctx:
        keep = ctx.enter_context(tc.tile_pool(name="keep", bufs=1))
        cast_pool = ctx.enter_context(tc.tile_pool(name="cast", bufs=4))
        grp_pool = ctx.enter_context(tc.tile_pool(name="grp", bufs=2))
        ep_pool = ctx.enter_context(tc.tile_pool(name="ep", bufs=4))
        st_pool = ctx.enter_context(tc.tile_pool(name="st", bufs=6))
        tp_pool = ctx.enter_context(tc.psum_pool(name="tp", bufs=2))
        u_pool = ctx.enter_context(tc.psum_pool(name="up", bufs=2))
        g_pool = ctx.enter_context(tc.psum_pool(name="gp", bufs=1))
        if MANUAL:
            ctx.enter_context(tc.manual_schedule())

        s8 = keep.tile([P, 8], F32, name="s8")
        wbytes = []
        x_sb = []
        for c in range(8):
            wbytes.append(keep.tile([P, 2, K], U8, name="wbytes%d" % c))
            x_sb.append(keep.tile([P, K], BF16, name="x_sb%d" % c))
        cos_t = []
        sin_t = []
        for pt in range(2):
            cos_t.append(keep.tile([P, DI], BF16, name="cos_t%d" % pt))
            sin_t.append(keep.tile([P, DI], BF16, name="sin_t%d" % pt))
        gain_row = keep.tile([P, DI], BF16, name="gain_row")
        gain_sb = keep.tile([P, DI], BF16, name="gain_sb")
        ones_bf = keep.tile([P, P], BF16, name="ones_bf")
        ident = keep.tile([P, P], F32, name="ident")
        warm = keep.tile([P, 1], F32, name="warm")
        gain_t = keep.tile([P, 8], F32, name="gain_t")
        gain_ps = {}

        def spread_gain():
            for s in range(2):
                bank = g_pool.tile([P, HALF], F32, tag="g%d" % s)
                gain_ps[s] = bank
                nc.tensor.matmul(
                    out=gain_ps[s][:], lhsT=ones_bf[:], rhs=gain_row[:, HALF * s : HALF * (s + 1)], start=True, stop=True
                )

        idle_rhs = keep.tile([P, HALF], BF16, name="idle_rhs")
        idle_ps = {}

        def keep_clock(count):
            for j in range(count):
                if j not in idle_ps:
                    bank = g_pool.tile([P, HALF], F32, tag="g%d" % j)
                    idle_ps[j] = bank
                nc.tensor.matmul(out=idle_ps[j][:], lhsT=ones_bf[:], rhs=idle_rhs[:], start=True, stop=True)

        x_codes = []
        x_scales = []
        w_codes = []
        w_scales = []
        for c in range(4):
            x_codes.append(keep.tile([P, 512], U32, name="x_codes%d" % c, align_bytes=64))
            x_scales.append(keep.tile([P, 512], U8, name="x_scales%d" % c, align_bytes=64))
            w_codes.append(keep.tile([P, 1024], U32, name="w_codes%d" % c, align_bytes=64))
            w_scales.append(keep.tile([P, 1024], U8, name="w_scales%d" % c, align_bytes=64))

        nc.vector.memset(warm[:], 1.0)
        nc.vector.memset(gain_row[:], 0.0)
        nc.vector.memset(ones_bf[:], 1.0)
        nc.vector.memset(idle_rhs[:], 0.0)
        make_identity(nc, ident[:])
        nc.scalar.dma_start(
            out=s8[:].rearrange("p (g t) -> p g t", t=4), in_=qk_w_scale.rearrange("o (g p t) -> p (o g) t", p=P, t=4)
        )
        nc.scalar.dma_start(out=gain_row[0:1, :], in_=sqk.rearrange("(o n) -> o n", o=1))
        nc.scalar.activation(out=warm[:], in_=warm[:], func=ACT.Abs_reciprocal_sqrt)

        def load_w(c):
            nc.sync.dma_start(out=wbytes[c][:], in_=w_pairs[c])

        def load_x(i):
            nc.sync.dma_start(out=x_sb[i][:], in_=x_flat[P * i : P * (i + 1), :])

        load_w(0)
        load_x(0)
        load_w(1)
        load_w(2)
        load_x(1)
        load_w(3)
        load_x(2)
        load_x(3)
        for i in range(4, 8):
            load_x(i)
        for pt in range(2):
            nc.sync.dma_start(out=cos_t[pt][:], in_=cos[P * pt : P * (pt + 1), :])
            nc.sync.dma_start(out=sin_t[pt][:], in_=sin[P * pt : P * (pt + 1), :])
        for c in range(4):
            load_w(4 + c)

        xg_tiles = {}
        x_banks = {}

        def turn_x(i):
            words = x_sb[i][:].bitcast(F32)
            bank = u_pool.tile([P, 2, 2, P], F32, tag=("u_lo", "u_hi")[i % 2])
            for g in range(2):
                for u in range(2):
                    nc.tensor.transpose(bank[:, g, u, :], words[:, 256 * g + u : 256 * (g + 1) : 2], ident[:])
            x_banks[i] = bank

        def evac_x(i):
            if i % 2 == 0:
                xg = grp_pool.tile([P, 2048], BF16, tag="xg", align_bytes=64, bufs=2)
                xg_tiles[i // 2] = xg
            nc.scalar.copy(
                out=xg_tiles[i // 2][:, 1024 * (i % 2) : 1024 * (i % 2 + 1)]
                .bitcast(F32)
                .rearrange("p (g r u) -> p g r u", g=2, u=2),
                in_=x_banks[i][:].rearrange("p g u r -> p g r u"),
            )

        def quant_x(pair):
            nc.vector.quantize_mx(out=x_codes[pair][:].bitcast(FP8X4), scales=x_scales[pair][:], in_=xg_tiles[pair][:])

        wbf_tiles = {}
        w_banks = {}
        wg_tiles = {}

        def cast_w(c):
            wbf = cast_pool.tile([P, 2, K], BF16, tag="wbf")
            if c in CAST_ON_VECTOR:
                nc.vector.tensor_copy(out=wbf[:], in_=wbytes[c][:].bitcast(FP8))
            else:
                nc.scalar.copy(out=wbf[:], in_=wbytes[c][:].bitcast(FP8))
            wbf_tiles[c] = wbf

        def turn_w(c, g):
            words = wbf_tiles[c][:].rearrange("p j k -> p (j k)").bitcast(F32).rearrange("p (j w) -> p j w", j=2)
            bank = tp_pool.tile([P, 2, 2, P], F32, tag="bank")
            for u in range(2):
                for jj in range(2):
                    nc.tensor.transpose(bank[:, u, jj, :], words[:, jj, 256 * g + u : 256 * (g + 1) : 2], ident[:])
            w_banks[(c, g)] = bank

        def scale_w(c, g):
            chunk, pos = divmod(c, 2)
            if pos == 0 and g == 0:
                wg = grp_pool.tile([P, 4096], BF16, tag="wg", align_bytes=64, bufs=2)
                wg_tiles[chunk] = wg
            src = w_banks[(c, g)][:].rearrange("p u j r -> p (u j r)").bitcast(BF16)
            dst = wg_tiles[chunk][:].rearrange("p (g n t) -> p g n t", g=2, t=4)
            nc.vector.tensor_tensor(
                out=dst[:, g, 256 * pos : 256 * (pos + 1), :].rearrange("p n (u e) -> p n u e", u=2),
                in0=src.rearrange("p (u n e) -> p n u e", u=2, e=2),
                in1=s8[:, 4 * g : 4 * (g + 1)].rearrange("p (u e) -> p u e", u=2).unsqueeze(1).to_broadcast([P, 256, 2, 2]),
                op=ALU.mult,
            )

        def quant_w(chunk):
            nc.vector.quantize_mx(out=w_codes[chunk][:].bitcast(FP8X4), scales=w_scales[chunk][:], in_=wg_tiles[chunk][:])

        u_tiles = {}

        def mm(n):
            h, i = divmod(n, 8)
            u_lo = u_pool.tile([P, HALF], F32, tag="u_lo")
            u_hi = u_pool.tile([P, HALF], F32, tag="u_hi")
            u_tiles[n] = (u_lo, u_hi)
            for half in range(2):
                for g in range(2):
                    nc.tensor.matmul_mx(
                        out=u_tiles[n][half][:],
                        lhsT=x_codes[i // 2][:, 256 * (i % 2) + P * g : 256 * (i % 2) + P * (g + 1)].bitcast(FP8X4),
                        lhsT_scale=x_scales[i // 2][:, 256 * (i % 2) + P * g : 256 * (i % 2) + P * (g + 1)],
                        rhs=w_codes[2 * h + half][:, HALF * g : HALF * (g + 1)].bitcast(FP8X4),
                        rhs_scale=w_scales[2 * h + half][:, HALF * g : HALF * (g + 1)],
                        start=(g == 0),
                        stop=(g == 1),
                    )

        r_tiles = {}
        rg_tiles = {}
        rn_tiles = {}
        o_tiles = {}

        def rope(n):
            pt = n % 2
            u_lo, u_hi = u_tiles[n]
            a = ep_pool.tile([P, DI], F32, tag="a", bufs=5)
            b = ep_pool.tile([P, DI], F32, tag="b", bufs=3)
            lo, hi = slice(0, HALF), slice(HALF, DI)
            nc.vector.tensor_tensor(out=a[:, lo], in0=u_lo[:], in1=cos_t[pt][:, lo], op=ALU.mult)
            if n == 15:
                nc.vector.scalar_tensor_tensor(
                    out=b[:, lo], in0=u_hi[:], scalar=-1.0, in1=sin_t[pt][:, lo], op0=ALU.mult, op1=ALU.mult
                )
                nc.vector.tensor_tensor(out=a[:, hi], in0=u_hi[:], in1=cos_t[pt][:, hi], op=ALU.mult)
                nc.vector.tensor_tensor(out=b[:, hi], in0=u_lo[:], in1=sin_t[pt][:, hi], op=ALU.mult)
                for half in (lo, hi):
                    nc.vector.tensor_tensor(out=a[:, half], in0=a[:, half], in1=b[:, half], op=ALU.add)
            else:
                nc.vector.tensor_tensor(out=b[:, hi], in0=u_lo[:], in1=sin_t[pt][:, hi], op=ALU.mult)
                nc.vector.tensor_tensor(out=a[:, hi], in0=u_hi[:], in1=cos_t[pt][:, hi], op=ALU.mult)
                nc.vector.scalar_tensor_tensor(
                    out=b[:, lo], in0=u_hi[:], scalar=-1.0, in1=sin_t[pt][:, lo], op0=ALU.mult, op1=ALU.mult
                )
                nc.gpsimd.tensor_tensor(out=a[:], in0=a[:], in1=b[:], op=ALU.add)
            r_tiles[n] = a
            if GM[n] > 0:
                rg = ep_pool.tile([P, DI], F32, tag="rg", bufs=3)
                cols = slice(DI - HALF * GM[n], DI)
                nc.gpsimd.tensor_tensor(out=rg[:, cols], in0=a[:, cols], in1=gain_sb[:, cols], op=ALU.mult)
                rg_tiles[n] = rg

        def norm(n):
            junk = ep_pool.tile([P, DI], BF16, tag="junk", bufs=2)
            rn = st_pool.tile([P, 1], F32, tag="rn")
            if n == 15:
                ss = st_pool.tile([P, 2], F32, tag="ss2", bufs=1)
                for s in range(2):
                    cols = slice(HALF * s, HALF * (s + 1))
                    nc.scalar.activation(
                        out=junk[:, cols], in_=r_tiles[n][:, cols], func=ACT.Square, scale=1.0 / 32.0, accum_out=ss[:, s : s + 1]
                    )
                nc.scalar.activation(
                    out=rn[:], in_=ss[:, 0:1], func=ACT.Abs_reciprocal_sqrt, bias=ss[:, 1:2], scale=1.0
                )
            else:
                ss = st_pool.tile([P, 1], F32, tag="ss")
                nc.scalar.activation(out=junk[:], in_=r_tiles[n][:], func=ACT.Square, accum_out=ss[:])
                nc.scalar.activation(out=rn[:], in_=ss[:], func=ACT.Abs_reciprocal_sqrt, scale=1.0 / 1024.0)
            rn_tiles[n] = rn

        def finish_scalar(n):
            o = ep_pool.tile([P, DI], F32, tag="o", bufs=4)
            o_tiles[n] = o
            if GM[n] > 0:
                lo = DI - HALF * GM[n]
                nc.scalar.activation(
                    out=o[:, lo:DI], in_=rg_tiles[n][:, lo:DI], func=ACT.Copy, scale=rn_tiles[n][:, 0:1]
                )

        t1_banks = {}
        t2_banks = {}
        rgt_tiles = {}

        def build_gain_t():
            bank = g_pool.tile([P, 8], F32, tag="g0")
            for c in range(8):
                nc.tensor.matmul(
                    out=bank[:, c : c + 1], lhsT=gain_row[:, P * c : P * (c + 1)], rhs=ones_bf[:, 0:1], start=True, stop=True
                )
            nc.scalar.copy(out=gain_t[:], in_=bank[:])

        ts_state = {"count": 1}

        def ts_bank(early):
            if early:
                k = ts_state["count"] % 2
                ts_state["count"] = ts_state["count"] + 1
                bank = g_pool.tile([P, 4, P], F32, tag="g%d" % k)
            else:
                bank = tp_pool.tile([P, 4, P], F32, tag="bank")
            return bank

        def t1(n, s, early):
            bank = ts_bank(early)
            for c in range(4):
                nc.tensor.transpose(bank[:, c, :], r_tiles[n][:, HALF * s + P * c : HALF * s + P * (c + 1)], ident[:])
            t1_banks[(n, s)] = bank

        def e1(n, s):
            rgt = ep_pool.tile([P, 4, P], F32, tag="rgt", bufs=4)
            for c in range(4):
                nc.scalar.activation(
                    out=rgt[:, c, :], in_=t1_banks[(n, s)][:, c, :], func=ACT.Copy, scale=gain_t[:, 4 * s + c : 4 * s + c + 1]
                )
            rgt_tiles[(n, s)] = rgt

        def t2(n, s, early):
            bank = ts_bank(early)
            for c in range(4):
                nc.tensor.transpose(bank[:, c, :], rgt_tiles[(n, s)][:, c, :], ident[:])
            t2_banks[(n, s)] = bank

        def e2(n, s):
            nc.scalar.activation(
                out=o_tiles[n][:, HALF * s : HALF * (s + 1)],
                in_=t2_banks[(n, s)][:].rearrange("p c r -> p (c r)"),
                func=ACT.Copy,
                scale=rn_tiles[n][:, 0:1],
            )

        def ts_round(m, f, s, early):
            do1 = m >= 0 and s < TS[m]
            do2 = f >= 0 and s < TS[f]
            if do1:
                t1(m, s, early)
            if do2:
                t2(f, s, early)
            if do1:
                e1(m, s)
            if do2:
                e2(f, s)

        def finish_vector(n):
            o = o_tiles[n]
            for s in range(TS[n], 2 - GM[n]):
                cols = slice(HALF * s, HALF * (s + 1))
                nc.vector.scalar_tensor_tensor(
                    out=o[:, cols], in0=r_tiles[n][:, cols], scalar=rn_tiles[n][:, 0:1], in1=gain_ps[s][:],
                    op0=ALU.mult, op1=ALU.mult,
                )

        def store(n):
            h, i = divmod(n, 8)
            rows = slice(P * i, P * (i + 1))
            o = o_tiles[n]
            if n >= 14:
                for s in range(2):
                    cols = slice(HALF * s, HALF * (s + 1))
                    nc.sync.dma_start(out=outs[h][rows, cols], in_=o[:, cols])
            else:
                nc.sync.dma_start(out=outs[h][rows, :], in_=o[:])

        jobs = []

        def job_x(i):
            jobs.append((lambda: turn_x(i), lambda: evac_x(i)))

        def job_w(c, g):
            jobs.append((lambda: turn_w(c, g), lambda: scale_w(c, g)))

        for c in range(8):
            job_w(c, 0)
            job_w(c, 1)
        state = {"made": 0, "used": 0}

        def make():
            if state["made"] < len(jobs):
                jobs[state["made"]][0]()
                state["made"] = state["made"] + 1

        def advance(count):
            for q in range(count):
                jobs[state["used"]][1]()
                state["used"] = state["used"] + 1
                make()

        def prep_x(i):
            if i <= 6:
                keep_clock(2)
            turn_x(i)
            evac_x(i)

        keep_clock(2)
        cast_w(0)
        turn_x(0)
        make()
        make()
        evac_x(0)
        cast_w(1)
        cast_w(2)
        prep_x(1)
        advance(2)
        cast_w(3)
        prep_x(2)
        advance(1)
        quant_x(0)
        prep_x(3)
        advance(1)
        quant_w(0)
        cast_w(4)
        prep_x(4)
        prep_x(5)
        advance(2)
        quant_x(1)
        prep_x(6)
        spread_gain()
        prep_x(7)
        advance(2)
        cast_w(5)
        nc.scalar.copy(out=gain_sb[:, HALF:DI], in_=gain_ps[1][:])
        quant_x(2)
        quant_w(1)
        mm(0)
        quant_x(3)
        mm(1)
        build_gain_t()
        cast_w(6)

        post = (1, 2, 1, 1, 1, 2)
        for n in range(16):
            f = n - FIN_LAG
            if f >= 0:
                finish_scalar(f)
            if n == 1:
                cast_w(7)
            rope(n)
            if n == 4:
                quant_w(2)
            if n == 6:
                quant_w(3)
            if n >= 1:
                norm(n - 1)
            ts_round(n - 1, f, 0, n <= LAST_EARLY)
            if n + 2 < 16:
                mm(n + 2)
            ts_round(n - 1, f, 1, n <= LAST_EARLY)
            if n == LAST_EARLY + 1:
                spread_gain()
            if f >= 0:
                finish_vector(f)
            if n < 6:
                advance(post[n])
            if f >= 0:
                store(f)
        norm(15)
        for n in range(16 - FIN_LAG, 16):
            finish_scalar(n)
            finish_vector(n)
            store(n)
